import numpy as np
import ml_dtypes


def mxq(x, axis, fmt="e4m3"):
    dtype, down = {"e4m3": (ml_dtypes.float8_e4m3fn, 7), "e5m2": (ml_dtypes.float8_e5m2, 14)}[fmt]
    v = np.moveaxis(np.asarray(x, np.float32).astype(ml_dtypes.bfloat16).astype(np.float64), axis, -1)
    blocks = v.reshape(v.shape[:-1] + (-1, 32))
    amax = np.abs(blocks).max(-1, keepdims=True)
    byte = np.maximum(np.where(amax > 0, np.frexp(amax)[1] - 1 + 127, 0) - down, 1)
    scale = np.exp2(byte - 127.0)
    codes = (blocks / scale).astype(np.float32).astype(dtype).astype(np.float64)
    return np.moveaxis((codes * scale).reshape(v.shape), -1, axis)


WIDE = False


def mx_kscale(k):
    if not WIDE:
        return np.ones(k)
    levels = np.array([10, -10, 5, -5, 0])
    if k % 512:
        return np.exp2(np.random.permutation(np.resize(levels, k // 32))).repeat(32)
    a = np.empty((k // 512, 16))
    for p in range(k // 512):
        a[p, :8] = np.random.permutation(np.resize(levels, 8))
        for g in range(8):
            far = levels[np.abs(levels - a[p, g]) >= 10]
            a[p, g + 8] = far[np.random.randint(len(far))]
    return np.exp2(a.ravel()).repeat(32)


BF16 = ml_dtypes.bfloat16


def bf(x):
    return np.asarray(x, np.float32).astype(BF16)


def f64(x):
    return np.asarray(x).astype(np.float64)


B, C, O, ROWS, COLS, KH, KW = 64, 64, 128, 8, 8, 4, 4
H, W, K = ROWS + KH - 1, COLS + KW - 1, C * KH * KW


def setup_inputs():
    sc = mx_kscale(K)[::KH * KW]
    return {"x": bf(np.random.standard_normal((B, C, H, W)) * sc[None, :, None, None]),
            "weight": bf(np.random.standard_normal((ROWS, COLS, O, C, KH, KW)) / np.sqrt(K) / sc[None, None, None, :, None, None])}


def reference(x, weight):
    x, weight = f64(x), f64(weight)
    rows, cols, o, c, kh, kw = weight.shape
    b = x.shape[0]
    patches = np.stack(
        [np.stack([x[:, :, u:u + rows, v:v + cols] for v in range(kw)], axis=2)
         for u in range(kh)], axis=2)
    p = patches.transpose(4, 5, 0, 1, 2, 3).reshape(rows * cols, b, c * kh * kw)
    w = weight.reshape(rows * cols, o, c * kh * kw)
    y = mxq(p, 2, "e4m3") @ mxq(w, 2, "e4m3").transpose(0, 2, 1)
    return y.reshape(rows, cols, b, o).transpose(2, 3, 0, 1)

@@ -1,0 +1,216 @@
+from contextlib import ExitStack
+
+import concourse.mybir as mybir
+from concourse.masks import make_identity
+
+F32 = mybir.dt.float32
+BF16 = mybir.dt.bfloat16
+I32 = mybir.dt.int32
+U32 = mybir.dt.uint32
+U8 = mybir.dt.uint8
+FP8X4 = mybir.dt.float8_e4m3fn_x4
+
+P = 128
+B, C, O, ROWS, COLS, KH, KW = 64, 64, 128, 8, 8, 4, 4
+H = 11
+CH = C // 2
+XLEN = CH * H * H
+K = C * KH * KW
+KP = K // 2
+NPOS = ROWS * COLS
+GRP = 4
+NG = NPOS // GRP
+NHR = 2 * ROWS
+WBUFS = 5
+LEAD = 1
+ROWW = COLS * P
+PAD = B
+EARLY_GROUPS = 12
+FLOPS = 2 * NPOS * B * O * K
+
+
+def tile_localconvolution_kernel(tc, x, weight, out):
+    nc = tc.nc
+    w_view = weight.rearrange("i j o c u v -> o (i j) (c u v)")
+    x_view = x.rearrange("b (g c) h w -> (b g) (c h w)", g=2)
+    out_view = out.rearrange("b o i j -> o b (i j)")
+
+    with ExitStack() as ctx:
+        keep = ctx.enter_context(tc.tile_pool(name="keep", bufs=1))
+        wraw_pool = ctx.enter_context(tc.tile_pool(name="wraw", bufs=WBUFS))
+        gw_pool = ctx.enter_context(tc.tile_pool(name="gw", bufs=3))
+        wq_pool = ctx.enter_context(tc.tile_pool(name="wq", bufs=6))
+        pi_pool = ctx.enter_context(tc.tile_pool(name="pi", bufs=3))
+        gp_pool = ctx.enter_context(tc.tile_pool(name="gp", bufs=2))
+        tp_pool = ctx.enter_context(tc.psum_pool(name="tp", bufs=6))
+        acc_pool = ctx.enter_context(tc.psum_pool(name="acc", bufs=2))
+        ctx.enter_context(tc.manual_schedule())
+
+        xs = keep.tile([P, XLEN], BF16, name="xs")
+        nc.sync.dma_start(out=xs[:], in_=x_view)
+        xs_img = xs[:].rearrange("p (c h w) -> p c h w", c=CH, h=H)
+
+        ident = keep.tile([P, P], F32, name="ident")
+        make_identity(nc, ident[:])
+        perm = keep.tile([P, P], F32, name="perm")
+        pc = keep.tile([P, ROWS, ROWW + PAD], U32, name="pc", align_bytes=64)
+        ps = keep.tile([P, ROWS, ROWW + PAD], U8, name="ps", align_bytes=64)
+        res = keep.tile([P, B, NPOS], F32, name="res")
+        nc.vector.memset(pc[:, :, ROWW:ROWW + PAD].bitcast(I32), 0)
+        nc.vector.memset(ps[:, :, ROWW:ROWW + PAD].bitcast(I32), 0)
+        nc.vector.tensor_copy(
+            out=perm[:].rearrange("p (g b) -> p g b", g=2),
+            in_=ident[:].rearrange("p (b g) -> p g b", g=2),
+        )
+
+        wraw = {}
+        gw = {}
+        wc = {}
+        ws = {}
+        pim = {}
+        gp = {}
+        accs = {}
+
+        def load_w(n):
+            t = wraw_pool.tile([P, GRP, K], BF16, name="wraw")
+            nc.sync.dma_start(out=t[:], in_=w_view[:, GRP * n:GRP * (n + 1), :])
+            wraw[n] = t
+
+        def flip(sources, matrix, view, dst_words, engine):
+            bank = tp_pool.tile([P, 512], F32, name="tp")
+            for s, src in enumerate(sources):
+                nc.tensor.transpose(bank[:, P * s:P * (s + 1)], src, matrix[:])
+            if engine == "s":
+                nc.scalar.copy(out=dst_words, in_=view(bank))
+            else:
+                nc.vector.tensor_copy(out=dst_words, in_=view(bank))
+
+        def w_view_of(bank):
+            return bank[:].rearrange("p (g m n) -> p g n m", g=2, m=2)
+
+        def p_view_of(bank):
+            return bank[:].rearrange("p (m n) -> p n m", m=2)
+
+        def group_flips(n):
+            wf = wraw[n][:].bitcast(F32)
+            g_t = gw_pool.tile([P, GRP, 2, O, 4], BF16, name="gw", align_bytes=64)
+            gw[n] = g_t
+            gf = g_t[:].bitcast(F32)
+            return [([wf[:, a, 2 * P * g + m:2 * P * (g + 1):2] for g in range(2) for m in range(2)], ident, w_view_of, gf[:, a], "s")
+                    for a in range(GRP)]
+
+        def quantise_group(n):
+            c_t = wq_pool.tile([P, GRP * 2 * O], U32, name="wc", align_bytes=64)
+            s_t = wq_pool.tile([P, GRP * 2 * O], U8, name="ws", align_bytes=64)
+            wc[n] = c_t
+            ws[n] = s_t
+            nc.vector.quantize_mx(
+                out=c_t[:].bitcast(FP8X4),
+                scales=s_t[:],
+                in_=gw[n][:].rearrange("p a g o t -> p (a g o t)"),
+            )
+
+        def im2col(hr):
+            i = hr // 2
+            t = pi_pool.tile([P, 2, 2, KP], BF16, name="pim")
+            pim[hr] = t
+            for e in range(2):
+                jr = 2 * (hr % 2) + e
+                nc.vector.tensor_copy(
+                    out=t[:, e].rearrange("p q (c u v) -> p c u q v", c=CH, u=KH),
+                    in_=xs_img[:, :, i:i + KH, jr:jr + 2 * KW].rearrange(
+                        "p c u (q v) -> p c u q v", q=2),
+                )
+
+        def half_row_flips(hr):
+            i = hr // 2
+            if hr % 2 == 0:
+                gp[i] = gp_pool.tile([P, COLS, 2, B, 4], BF16, name="gp", align_bytes=64)
+            gf = gp[i][:].bitcast(F32)
+            pf = pim[hr][:].bitcast(F32)
+            flips = []
+            for e in range(2):
+                jr = 2 * (hr % 2) + e
+                flips.append((
+                    [pf[:, e, q, m:2 * P:2] for m in range(2) for q in range(2)],
+                    perm, p_view_of,
+                    gf[:, 2 * jr:2 * jr + 2].rearrange("p a g b m -> p (a g b) m"),
+                    "s" if e == 0 else "v",
+                ))
+            return flips
+
+        def quantise_row(i):
+            nc.vector.quantize_mx(
+                out=pc[:, i, 0:ROWW].bitcast(FP8X4),
+                scales=ps[:, i, 0:ROWW],
+                in_=gp[i][:].rearrange("p a g b t -> p (a g b t)"),
+            )
+
+        def multiply_position(pos):
+            n, a = pos // GRP, pos % GRP
+            i, jh = n // 2, n % 2
+            if a == 0:
+                accs[n] = acc_pool.tile([P, 512], F32, name="acc")
+            acc = accs[n]
+            for a in range(a, a + 1):
+                for g in range(2):
+                    lo = (2 * a + g) * O
+                    col = P * (2 * a + jh) + B * g
+                    nc.tensor.matmul_mx(
+                        out=acc[:, P * a:P * (a + 1)],
+                        lhsT=wc[n][:, lo:lo + O].bitcast(FP8X4),
+                        lhsT_scale=ws[n][:, lo:lo + O],
+                        rhs=pc[:, i, col:col + P].bitcast(FP8X4),
+                        rhs_scale=ps[:, i, col:col + P],
+                        start=(g == 0),
+                        stop=(g == 1),
+                    )
+            if pos % GRP == GRP - 1:
+                nc.scalar.copy(
+                    out=res[:, :, GRP * n:GRP * (n + 1)],
+                    in_=acc[:].rearrange("p (a h b) -> p h b a", a=GRP, h=2)[:, 0],
+                )
+                if n + 1 == EARLY_GROUPS:
+                    nc.sync.dma_start(out=out_view[:, :, 0:done], in_=res[:, :, 0:done])
+
+        for n in range(WBUFS):
+            load_w(n)
+        im2col(0)
+
+        banks_done = 0
+        pos_done = 0
+        row_step = {}
+        pending_rows = []
+        done = GRP * EARLY_GROUPS
+        for t in range(NG + LEAD + 3):
+            w = t - LEAD
+            if 1 <= w <= NG:
+                quantise_group(w - 1)
+            for i in pending_rows:
+                quantise_row(i)
+                row_step[i] = t
+            pending_rows = []
+            if t + 1 < NHR:
+                im2col(t + 1)
+            flips = []
+            if 0 <= w < NG:
+                flips.extend(group_flips(w))
+            if t < NHR:
+                flips.extend(half_row_flips(t))
+                if t % 2 == 1:
+                    pending_rows.append(t // 2)
+            for sources, matrix, view, dst_w, eng in flips:
+                flip(sources, matrix, view, dst_w, eng)
+                banks_done += 1
+                if banks_done % 4 == 0:
+                    while pos_done < (2 * banks_done - 28) // 3:
+                        multiply_position(pos_done)
+                        pos_done += 1
+            if w >= NG - 1:
+                while pos_done < min(NPOS, GRP * (t - 2)):
+                    multiply_position(pos_done)
+                    pos_done += 1
+            if 0 <= w < NG and w + WBUFS < NG:
+                load_w(w + WBUFS)
+
+        nc.sync.dma_start(out=out_view[:, :, done:NPOS], in_=res[:, :, done:NPOS])

@@ -16,14 +16,12 @@ H = 11
 CH = C // 2
 XLEN = CH * H * H
 K = C * KH * KW
-KP = K // 2
 NPOS = ROWS * COLS
 GRP = 4
 NG = NPOS // GRP
-NHR = 2 * ROWS
+SPAN = 8
 WBUFS = 5
-LEAD = 1
-ROWW = COLS * P
+GCOLS = GRP * P
 PAD = B
 EARLY_GROUPS = 12
 FLOPS = 2 * NPOS * B * O * K
@@ -39,9 +37,10 @@ def tile_localconvolution_kernel(tc, x, weight, out):
         keep = ctx.enter_context(tc.tile_pool(name="keep", bufs=1))
         wraw_pool = ctx.enter_context(tc.tile_pool(name="wraw", bufs=WBUFS))
         gw_pool = ctx.enter_context(tc.tile_pool(name="gw", bufs=3))
-        wq_pool = ctx.enter_context(tc.tile_pool(name="wq", bufs=6))
-        pi_pool = ctx.enter_context(tc.tile_pool(name="pi", bufs=3))
-        gp_pool = ctx.enter_context(tc.tile_pool(name="gp", bufs=2))
+        wq_pool = ctx.enter_context(tc.tile_pool(name="wq", bufs=5))
+        pre_pool = ctx.enter_context(tc.tile_pool(name="pre", bufs=3))
+        xt_pool = ctx.enter_context(tc.tile_pool(name="xt", bufs=3))
+        gp_pool = ctx.enter_context(tc.tile_pool(name="gp", bufs=3))
         tp_pool = ctx.enter_context(tc.psum_pool(name="tp", bufs=6))
         acc_pool = ctx.enter_context(tc.psum_pool(name="acc", bufs=2))
         ctx.enter_context(tc.manual_schedule())
@@ -53,53 +52,36 @@ def tile_localconvolution_kernel(tc, x, weight, out):
         ident = keep.tile([P, P], F32, name="ident")
         make_identity(nc, ident[:])
         perm = keep.tile([P, P], F32, name="perm")
-        pc = keep.tile([P, ROWS, ROWW + PAD], U32, name="pc", align_bytes=64)
-        ps = keep.tile([P, ROWS, ROWW + PAD], U8, name="ps", align_bytes=64)
+        pc = keep.tile([P, NG, GCOLS + PAD], U32, name="pc", align_bytes=64)
+        ps = keep.tile([P, NG, GCOLS + PAD], U8, name="ps", align_bytes=64)
         res = keep.tile([P, B, NPOS], F32, name="res")
-        nc.vector.memset(pc[:, :, ROWW:ROWW + PAD].bitcast(I32), 0)
-        nc.vector.memset(ps[:, :, ROWW:ROWW + PAD].bitcast(I32), 0)
+        nc.vector.memset(pc[:, :, GCOLS:GCOLS + PAD].bitcast(I32), 0)
+        nc.vector.memset(ps[:, :, GCOLS:GCOLS + PAD].bitcast(I32), 0)
         nc.vector.tensor_copy(
             out=perm[:].rearrange("p (g b) -> p g b", g=2),
             in_=ident[:].rearrange("p (b g) -> p g b", g=2),
         )
 
-        wraw = {}
-        gw = {}
-        wc = {}
-        ws = {}
-        pim = {}
-        gp = {}
-        accs = {}
+        wraw, gw, wc, ws, pre, xt, gp, accs = {}, {}, {}, {}, {}, {}, {}, {}
 
         def load_w(n):
             t = wraw_pool.tile([P, GRP, K], BF16, name="wraw")
             nc.sync.dma_start(out=t[:], in_=w_view[:, GRP * n:GRP * (n + 1), :])
             wraw[n] = t
 
-        def flip(sources, matrix, view, dst_words, engine):
-            bank = tp_pool.tile([P, 512], F32, name="tp")
-            for s, src in enumerate(sources):
-                nc.tensor.transpose(bank[:, P * s:P * (s + 1)], src, matrix[:])
-            if engine == "s":
-                nc.scalar.copy(out=dst_words, in_=view(bank))
-            else:
-                nc.vector.tensor_copy(out=dst_words, in_=view(bank))
-
-        def w_view_of(bank):
-            return bank[:].rearrange("p (g m n) -> p g n m", g=2, m=2)
-
-        def p_view_of(bank):
-            return bank[:].rearrange("p (m n) -> p n m", m=2)
-
-        def group_flips(n):
+        def flip_w(n, a):
+            if a == 0:
+                gw[n] = gw_pool.tile([P, GRP, 2, O, 4], BF16, name="gw", align_bytes=64)
             wf = wraw[n][:].bitcast(F32)
-            g_t = gw_pool.tile([P, GRP, 2, O, 4], BF16, name="gw", align_bytes=64)
-            gw[n] = g_t
-            gf = g_t[:].bitcast(F32)
-            return [([wf[:, a, 2 * P * g + m:2 * P * (g + 1):2] for g in range(2) for m in range(2)], ident, w_view_of, gf[:, a], "s")
-                    for a in range(GRP)]
+            gf = gw[n][:].bitcast(F32)
+            bank = tp_pool.tile([P, 512], F32, name="tp")
+            for s in range(4):
+                g, m = s // 2, s % 2
+                nc.tensor.transpose(bank[:, P * s:P * (s + 1)],
+                                    wf[:, a, 2 * P * g + m:2 * P * (g + 1):2], ident[:])
+            nc.scalar.copy(out=gf[:, a], in_=bank[:].rearrange("p (g m n) -> p g n m", g=2, m=2))
 
-        def quantise_group(n):
+        def quantise_w(n):
             c_t = wq_pool.tile([P, GRP * 2 * O], U32, name="wc", align_bytes=64)
             s_t = wq_pool.tile([P, GRP * 2 * O], U8, name="ws", align_bytes=64)
             wc[n] = c_t
@@ -110,107 +92,86 @@ def tile_localconvolution_kernel(tc, x, weight, out):
                 in_=gw[n][:].rearrange("p a g o t -> p (a g o t)"),
             )
 
-        def im2col(hr):
-            i = hr // 2
-            t = pi_pool.tile([P, 2, 2, KP], BF16, name="pim")
-            pim[hr] = t
-            for e in range(2):
-                jr = 2 * (hr % 2) + e
-                nc.vector.tensor_copy(
-                    out=t[:, e].rearrange("p q (c u v) -> p c u q v", c=CH, u=KH),
-                    in_=xs_img[:, :, i:i + KH, jr:jr + 2 * KW].rearrange(
-                        "p c u (q v) -> p c u q v", q=2),
-                )
+        def first_col(n):
+            return (n % 2) * 3
 
-        def half_row_flips(hr):
-            i = hr // 2
-            if hr % 2 == 0:
-                gp[i] = gp_pool.tile([P, COLS, 2, B, 4], BF16, name="gp", align_bytes=64)
-            gf = gp[i][:].bitcast(F32)
-            pf = pim[hr][:].bitcast(F32)
-            flips = []
-            for e in range(2):
-                jr = 2 * (hr % 2) + e
-                flips.append((
-                    [pf[:, e, q, m:2 * P:2] for m in range(2) for q in range(2)],
-                    perm, p_view_of,
-                    gf[:, 2 * jr:2 * jr + 2].rearrange("p a g b m -> p (a g b) m"),
-                    "s" if e == 0 else "v",
-                ))
-            return flips
-
-        def quantise_row(i):
-            nc.vector.quantize_mx(
-                out=pc[:, i, 0:ROWW].bitcast(FP8X4),
-                scales=ps[:, i, 0:ROWW],
-                in_=gp[i][:].rearrange("p a g b t -> p (a g b t)"),
+        def gather_windows(n):
+            i, w0 = n // 2, first_col(n)
+            t = pre_pool.tile([P, GRP, P, 2], BF16, name="pre")
+            pre[n] = t
+            nc.vector.tensor_copy(
+                out=t[:].rearrange("p m (c u) e -> p c u m e", u=KH),
+                in_=xs_img[:, :, i:i + KH, w0:w0 + SPAN].rearrange("p c u (m e) -> p c u m e", e=2),
             )
 
-        def multiply_position(pos):
-            n, a = pos // GRP, pos % GRP
-            i, jh = n // 2, n % 2
-            if a == 0:
-                accs[n] = acc_pool.tile([P, 512], F32, name="acc")
-            acc = accs[n]
-            for a in range(a, a + 1):
+        def flip_x(n):
+            pf = pre[n][:].bitcast(F32).rearrange("p m q e -> p m (q e)")
+            bank = tp_pool.tile([P, 512], F32, name="tp")
+            for m in range(4):
+                nc.tensor.transpose(bank[:, P * m:P * (m + 1)], pf[:, m], perm[:])
+            t = xt_pool.tile([P, P, SPAN], BF16, name="xt", align_bytes=64)
+            xt[n] = t
+            nc.scalar.copy(out=t[:].bitcast(F32), in_=bank[:].rearrange("p (m n) -> p n m", m=4))
+
+        def spread_patches(n):
+            w0 = first_col(n)
+            t = gp_pool.tile([P, GRP, P, KW], BF16, name="gp", align_bytes=64)
+            gp[n] = t
+            for a in range(GRP):
+                lo = GRP * (n % 2) + a - w0
+                nc.vector.tensor_copy(out=t[:, a], in_=xt[n][:, :, lo:lo + KW])
+
+        def quantise_p(n):
+            nc.vector.quantize_mx(
+                out=pc[:, n, 0:GCOLS].bitcast(FP8X4),
+                scales=ps[:, n, 0:GCOLS],
+                in_=gp[n][:].rearrange("p a n t -> p (a n t)"),
+            )
+
+        def multiply(n):
+            acc = acc_pool.tile([P, 512], F32, name="acc")
+            for a in range(GRP):
                 for g in range(2):
                     lo = (2 * a + g) * O
-                    col = P * (2 * a + jh) + B * g
+                    col = P * a + B * g
                     nc.tensor.matmul_mx(
                         out=acc[:, P * a:P * (a + 1)],
                         lhsT=wc[n][:, lo:lo + O].bitcast(FP8X4),
                         lhsT_scale=ws[n][:, lo:lo + O],
-                        rhs=pc[:, i, col:col + P].bitcast(FP8X4),
-                        rhs_scale=ps[:, i, col:col + P],
+                        rhs=pc[:, n, col:col + P].bitcast(FP8X4),
+                        rhs_scale=ps[:, n, col:col + P],
                         start=(g == 0),
                         stop=(g == 1),
                     )
-            if pos % GRP == GRP - 1:
-                nc.scalar.copy(
-                    out=res[:, :, GRP * n:GRP * (n + 1)],
-                    in_=acc[:].rearrange("p (a h b) -> p h b a", a=GRP, h=2)[:, 0],
-                )
-                if n + 1 == EARLY_GROUPS:
-                    nc.sync.dma_start(out=out_view[:, :, 0:done], in_=res[:, :, 0:done])
+            nc.scalar.copy(
+                out=res[:, :, GRP * n:GRP * (n + 1)],
+                in_=acc[:].rearrange("p (a h b) -> p h b a", a=GRP, h=2)[:, 0],
+            )
 
         for n in range(WBUFS):
             load_w(n)
-        im2col(0)
+        gather_windows(0)
 
-        banks_done = 0
-        pos_done = 0
-        row_step = {}
-        pending_rows = []
         done = GRP * EARLY_GROUPS
-        for t in range(NG + LEAD + 3):
-            w = t - LEAD
-            if 1 <= w <= NG:
-                quantise_group(w - 1)
-            for i in pending_rows:
-                quantise_row(i)
-                row_step[i] = t
-            pending_rows = []
-            if t + 1 < NHR:
-                im2col(t + 1)
-            flips = []
-            if 0 <= w < NG:
-                flips.extend(group_flips(w))
-            if t < NHR:
-                flips.extend(half_row_flips(t))
-                if t % 2 == 1:
-                    pending_rows.append(t // 2)
-            for sources, matrix, view, dst_w, eng in flips:
-                flip(sources, matrix, view, dst_w, eng)
-                banks_done += 1
-                if banks_done % 4 == 0:
-                    while pos_done < (2 * banks_done - 28) // 3:
-                        multiply_position(pos_done)
-                        pos_done += 1
-            if w >= NG - 1:
-                while pos_done < min(NPOS, GRP * (t - 2)):
-                    multiply_position(pos_done)
-                    pos_done += 1
-            if 0 <= w < NG and w + WBUFS < NG:
-                load_w(w + WBUFS)
+        for t in range(NG + 3):
+            if 0 <= t - 2 < NG:
+                quantise_p(t - 2)
+            if 0 <= t - 1 < NG:
+                spread_patches(t - 1)
+            if 0 <= t - 2 < NG:
+                quantise_w(t - 2)
+            if t + 1 < NG:
+                gather_windows(t + 1)
+            if t < NG:
+                flip_x(t)
+            for a in range(GRP):
+                if 0 <= t - 1 < NG:
+                    flip_w(t - 1, a)
+                if a == 1 and 0 <= t - 3 < NG:
+                    multiply(t - 3)
+            if t - 3 == EARLY_GROUPS - 1:
+                nc.sync.dma_start(out=out_view[:, :, 0:done], in_=res[:, :, 0:done])
+            if 0 <= t - 1 and t - 1 + WBUFS < NG:
+                load_w(t - 1 + WBUFS)
 
         nc.sync.dma_start(out=out_view[:, :, done:NPOS], in_=res[:, :, done:NPOS])

@@ -21,8 +21,8 @@ GRP = 4
 NG = NPOS // GRP
 SPAN = 8
 WBUFS = 5
-GCOLS = GRP * P
-PAD = B
+HALF = P * SPAN
+XT_LEN = 2 * HALF + 64
 EARLY_GROUPS = 12
 FLOPS = 2 * NPOS * B * O * K
 
@@ -40,7 +40,8 @@ def tile_localconvolution_kernel(tc, x, weight, out):
         wq_pool = ctx.enter_context(tc.tile_pool(name="wq", bufs=5))
         pre_pool = ctx.enter_context(tc.tile_pool(name="pre", bufs=3))
         xt_pool = ctx.enter_context(tc.tile_pool(name="xt", bufs=3))
-        gp_pool = ctx.enter_context(tc.tile_pool(name="gp", bufs=3))
+        sp_pool = ctx.enter_context(tc.tile_pool(name="sp", bufs=2))
+        pq_pool = ctx.enter_context(tc.tile_pool(name="pq", bufs=3))
         tp_pool = ctx.enter_context(tc.psum_pool(name="tp", bufs=6))
         acc_pool = ctx.enter_context(tc.psum_pool(name="acc", bufs=2))
         ctx.enter_context(tc.manual_schedule())
@@ -52,17 +53,13 @@ def tile_localconvolution_kernel(tc, x, weight, out):
         ident = keep.tile([P, P], F32, name="ident")
         make_identity(nc, ident[:])
         perm = keep.tile([P, P], F32, name="perm")
-        pc = keep.tile([P, NG, GCOLS + PAD], U32, name="pc", align_bytes=64)
-        ps = keep.tile([P, NG, GCOLS + PAD], U8, name="ps", align_bytes=64)
         res = keep.tile([P, B, NPOS], F32, name="res")
-        nc.vector.memset(pc[:, :, GCOLS:GCOLS + PAD].bitcast(I32), 0)
-        nc.vector.memset(ps[:, :, GCOLS:GCOLS + PAD].bitcast(I32), 0)
         nc.vector.tensor_copy(
             out=perm[:].rearrange("p (g b) -> p g b", g=2),
             in_=ident[:].rearrange("p (b g) -> p g b", g=2),
         )
 
-        wraw, gw, wc, ws, pre, xt, gp, accs = {}, {}, {}, {}, {}, {}, {}, {}
+        wraw, gw, wc, ws, pre, xt, sp, pc, ps = {}, {}, {}, {}, {}, {}, {}, {}, {}
 
         def load_w(n):
             t = wraw_pool.tile([P, GRP, K], BF16, name="wraw")
@@ -109,43 +106,54 @@ def tile_localconvolution_kernel(tc, x, weight, out):
             bank = tp_pool.tile([P, 512], F32, name="tp")
             for m in range(4):
                 nc.tensor.transpose(bank[:, P * m:P * (m + 1)], pf[:, m], perm[:])
-            t = xt_pool.tile([P, P, SPAN], BF16, name="xt", align_bytes=64)
-            xt[n] = t
-            nc.scalar.copy(out=t[:].bitcast(F32), in_=bank[:].rearrange("p (m n) -> p n m", m=4))
-
-        def spread_patches(n):
-            w0 = first_col(n)
-            t = gp_pool.tile([P, GRP, P, KW], BF16, name="gp", align_bytes=64)
-            gp[n] = t
-            for a in range(GRP):
-                lo = GRP * (n % 2) + a - w0
-                nc.vector.tensor_copy(out=t[:, a], in_=xt[n][:, :, lo:lo + KW])
-
-        def quantise_p(n):
-            nc.vector.quantize_mx(
-                out=pc[:, n, 0:GCOLS].bitcast(FP8X4),
-                scales=ps[:, n, 0:GCOLS],
-                in_=gp[n][:].rearrange("p a n t -> p (a n t)"),
+            i, h = n // 2, n % 2
+            if h == 0:
+                xt[i] = xt_pool.tile([P, XT_LEN], BF16, name="xt", align_bytes=64)
+            nc.scalar.copy(
+                out=xt[i][:, HALF * h:HALF * (h + 1)].bitcast(F32).rearrange("p (n m) -> p n m", m=4),
+                in_=bank[:].rearrange("p (m n) -> p n m", m=4),
             )
 
+        def spread(i):
+            t = sp_pool.tile([P, 2, P, 2, KW], BF16, name="sp", align_bytes=64)
+            sp[i] = t
+            for k in range(2):
+                lo = k + 1
+                nc.vector.tensor_copy(
+                    out=t[:, k],
+                    in_=xt[i][:, lo:lo + 2 * (HALF + 1)].rearrange("p (h x) -> p h x", h=2)[
+                        :, :, 0:HALF].rearrange("p h (n e) -> p n h e", e=SPAN)[:, :, :, 0:KW],
+                )
+
+        def quantise_p(i, kind):
+            if kind == 0:
+                pc[i] = pq_pool.tile([P, 2, 4 * P], U32, name="pc", align_bytes=64)
+                ps[i] = pq_pool.tile([P, 2, 4 * P], U8, name="ps", align_bytes=64)
+                src = xt[i][:, 0:2 * HALF]
+            else:
+                src = sp[i][:].rearrange("p k n q v -> p (k n q v)")
+            nc.vector.quantize_mx(out=pc[i][:, kind].bitcast(FP8X4), scales=ps[i][:, kind], in_=src)
+
         def multiply(n):
+            i, q = n // 2, n % 2
             acc = acc_pool.tile([P, 512], F32, name="acc")
             for a in range(GRP):
+                kind, k = ((0, 0), (1, 0), (1, 1), (0, 1))[a]
                 for g in range(2):
                     lo = (2 * a + g) * O
-                    col = P * a + B * g
+                    col = 2 * P * k + P * g
                     nc.tensor.matmul_mx(
                         out=acc[:, P * a:P * (a + 1)],
                         lhsT=wc[n][:, lo:lo + O].bitcast(FP8X4),
                         lhsT_scale=ws[n][:, lo:lo + O],
-                        rhs=pc[:, n, col:col + P].bitcast(FP8X4),
-                        rhs_scale=ps[:, n, col:col + P],
+                        rhs=pc[i][:, kind, col:col + P].bitcast(FP8X4),
+                        rhs_scale=ps[i][:, kind, col:col + P],
                         start=(g == 0),
                         stop=(g == 1),
                     )
             nc.scalar.copy(
                 out=res[:, :, GRP * n:GRP * (n + 1)],
-                in_=acc[:].rearrange("p (a h b) -> p h b a", a=GRP, h=2)[:, 0],
+                in_=acc[:].rearrange("p (a b q) -> p q b a", a=GRP, q=2)[:, q],
             )
 
         for n in range(WBUFS):
@@ -154,10 +162,11 @@ def tile_localconvolution_kernel(tc, x, weight, out):
 
         done = GRP * EARLY_GROUPS
         for t in range(NG + 3):
-            if 0 <= t - 2 < NG:
-                quantise_p(t - 2)
-            if 0 <= t - 1 < NG:
-                spread_patches(t - 1)
+            if t >= 2 and t % 2 == 0 and t // 2 - 1 < ROWS:
+                quantise_p(t // 2 - 1, 0)
+                spread(t // 2 - 1)
+            if t >= 3 and t % 2 == 1 and t // 2 - 1 < ROWS:
+                quantise_p(t // 2 - 1, 1)
             if 0 <= t - 2 < NG:
                 quantise_w(t - 2)
             if t + 1 < NG:

@@ -21,6 +21,7 @@ GRP = 4
 NG = NPOS // GRP
 SPAN = 8
 WBUFS = 5
+LEAD = 2
 HALF = P * SPAN
 XT_LEN = 2 * HALF + 64
 EARLY_GROUPS = 12
@@ -37,8 +38,8 @@ def tile_localconvolution_kernel(tc, x, weight, out):
         keep = ctx.enter_context(tc.tile_pool(name="keep", bufs=1))
         wraw_pool = ctx.enter_context(tc.tile_pool(name="wraw", bufs=WBUFS))
         gw_pool = ctx.enter_context(tc.tile_pool(name="gw", bufs=3))
-        wq_pool = ctx.enter_context(tc.tile_pool(name="wq", bufs=5))
-        pre_pool = ctx.enter_context(tc.tile_pool(name="pre", bufs=3))
+        wq_pool = ctx.enter_context(tc.tile_pool(name="wq", bufs=8))
+        pre_pool = ctx.enter_context(tc.tile_pool(name="pre", bufs=4))
         xt_pool = ctx.enter_context(tc.tile_pool(name="xt", bufs=3))
         sp_pool = ctx.enter_context(tc.tile_pool(name="sp", bufs=2))
         pq_pool = ctx.enter_context(tc.tile_pool(name="pq", bufs=3))
@@ -78,15 +79,15 @@ def tile_localconvolution_kernel(tc, x, weight, out):
                                     wf[:, a, 2 * P * g + m:2 * P * (g + 1):2], ident[:])
             nc.scalar.copy(out=gf[:, a], in_=bank[:].rearrange("p (g m n) -> p g n m", g=2, m=2))
 
-        def quantise_w(n):
-            c_t = wq_pool.tile([P, GRP * 2 * O], U32, name="wc", align_bytes=64)
-            s_t = wq_pool.tile([P, GRP * 2 * O], U8, name="ws", align_bytes=64)
-            wc[n] = c_t
-            ws[n] = s_t
+        def quantise_w(n, pair):
+            c_t = wq_pool.tile([P, 2 * 2 * O], U32, name="wc", align_bytes=64)
+            s_t = wq_pool.tile([P, 2 * 2 * O], U8, name="ws", align_bytes=64)
+            wc[n, pair] = c_t
+            ws[n, pair] = s_t
             nc.vector.quantize_mx(
                 out=c_t[:].bitcast(FP8X4),
                 scales=s_t[:],
-                in_=gw[n][:].rearrange("p a g o t -> p (a g o t)"),
+                in_=gw[n][:, 2 * pair:2 * pair + 2].rearrange("p a g o t -> p (a g o t)"),
             )
 
         def first_col(n):
@@ -102,17 +103,18 @@ def tile_localconvolution_kernel(tc, x, weight, out):
             )
 
         def flip_x(n):
+            i, h = n // 2, n % 2
             pf = pre[n][:].bitcast(F32).rearrange("p m q e -> p m (q e)")
             bank = tp_pool.tile([P, 512], F32, name="tp")
             for m in range(4):
                 nc.tensor.transpose(bank[:, P * m:P * (m + 1)], pf[:, m], perm[:])
-            i, h = n // 2, n % 2
             if h == 0:
                 xt[i] = xt_pool.tile([P, XT_LEN], BF16, name="xt", align_bytes=64)
-            nc.scalar.copy(
-                out=xt[i][:, HALF * h:HALF * (h + 1)].bitcast(F32).rearrange("p (n m) -> p n m", m=4),
-                in_=bank[:].rearrange("p (m n) -> p n m", m=4),
-            )
+            words = xt[i][:, HALF * h:HALF * (h + 1)].bitcast(F32).rearrange("p (n m) -> p n m", m=4)
+            if h == 0:
+                nc.scalar.copy(out=words, in_=bank[:].rearrange("p (m n) -> p n m", m=4))
+            else:
+                nc.vector.tensor_copy(out=words, in_=bank[:].rearrange("p (m n) -> p n m", m=4))
 
         def spread(i):
             t = sp_pool.tile([P, 2, P, 2, KW], BF16, name="sp", align_bytes=64)
@@ -140,12 +142,12 @@ def tile_localconvolution_kernel(tc, x, weight, out):
             for a in range(GRP):
                 kind, k = ((0, 0), (1, 0), (1, 1), (0, 1))[a]
                 for g in range(2):
-                    lo = (2 * a + g) * O
+                    lo = (2 * (a % 2) + g) * O
                     col = 2 * P * k + P * g
                     nc.tensor.matmul_mx(
                         out=acc[:, P * a:P * (a + 1)],
-                        lhsT=wc[n][:, lo:lo + O].bitcast(FP8X4),
-                        lhsT_scale=ws[n][:, lo:lo + O],
+                        lhsT=wc[n, a // 2][:, lo:lo + O].bitcast(FP8X4),
+                        lhsT_scale=ws[n, a // 2][:, lo:lo + O],
                         rhs=pc[i][:, kind, col:col + P].bitcast(FP8X4),
                         rhs_scale=ps[i][:, kind, col:col + P],
                         start=(g == 0),
@@ -159,28 +161,31 @@ def tile_localconvolution_kernel(tc, x, weight, out):
         for n in range(WBUFS):
             load_w(n)
         gather_windows(0)
+        gather_windows(1)
 
         done = GRP * EARLY_GROUPS
-        for t in range(NG + 3):
+        for t in range(NG + LEAD + 2):
+            w = t - LEAD
             if t >= 2 and t % 2 == 0 and t // 2 - 1 < ROWS:
                 quantise_p(t // 2 - 1, 0)
                 spread(t // 2 - 1)
             if t >= 3 and t % 2 == 1 and t // 2 - 1 < ROWS:
                 quantise_p(t // 2 - 1, 1)
-            if 0 <= t - 2 < NG:
-                quantise_w(t - 2)
-            if t + 1 < NG:
-                gather_windows(t + 1)
+            if t + 2 < NG:
+                gather_windows(t + 2)
             if t < NG:
                 flip_x(t)
+            if 0 <= w - 1 < NG:
+                quantise_w(w - 1, 0)
+                quantise_w(w - 1, 1)
             for a in range(GRP):
-                if 0 <= t - 1 < NG:
-                    flip_w(t - 1, a)
-                if a == 1 and 0 <= t - 3 < NG:
-                    multiply(t - 3)
-            if t - 3 == EARLY_GROUPS - 1:
+                if 0 <= w < NG:
+                    flip_w(w, a)
+                if a == 1 and 0 <= w - 2 < NG:
+                    multiply(w - 2)
+            if w - 2 == EARLY_GROUPS - 1:
                 nc.sync.dma_start(out=out_view[:, :, 0:done], in_=res[:, :, 0:done])
-            if 0 <= t - 1 and t - 1 + WBUFS < NG:
-                load_w(t - 1 + WBUFS)
+            if 0 <= w and w + WBUFS < NG:
+                load_w(w + WBUFS)
 
         nc.sync.dma_start(out=out_view[:, :, done:NPOS], in_=res[:, :, done:NPOS])

@@ -24,7 +24,7 @@ WBUFS = 5
 LEAD = 2
 HALF = P * SPAN
 XT_LEN = 2 * HALF + 64
-EARLY_GROUPS = 12
+LATE_ROWS = 2
 FLOPS = 2 * NPOS * B * O * K
 
 
@@ -62,9 +62,12 @@ def tile_localconvolution_kernel(tc, x, weight, out):
 
         wraw, gw, wc, ws, pre, xt, sp, pc, ps = {}, {}, {}, {}, {}, {}, {}, {}, {}
 
+        def group(n):
+            return (n + 2 * LATE_ROWS) % NG
+
         def load_w(n):
             t = wraw_pool.tile([P, GRP, K], BF16, name="wraw")
-            nc.sync.dma_start(out=t[:], in_=w_view[:, GRP * n:GRP * (n + 1), :])
+            nc.sync.dma_start(out=t[:], in_=w_view[:, GRP * group(n):GRP * (group(n) + 1), :])
             wraw[n] = t
 
         def flip_w(n, a):
@@ -94,7 +97,7 @@ def tile_localconvolution_kernel(tc, x, weight, out):
             return (n % 2) * 3
 
         def gather_windows(n):
-            i, w0 = n // 2, first_col(n)
+            i, w0 = group(n) // 2, first_col(n)
             t = pre_pool.tile([P, GRP, P, 2], BF16, name="pre")
             pre[n] = t
             nc.vector.tensor_copy(
@@ -154,7 +157,7 @@ def tile_localconvolution_kernel(tc, x, weight, out):
                         stop=(g == 1),
                     )
             nc.scalar.copy(
-                out=res[:, :, GRP * n:GRP * (n + 1)],
+                out=res[:, :, GRP * group(n):GRP * (group(n) + 1)],
                 in_=acc[:].rearrange("p (a b q) -> p q b a", a=GRP, q=2)[:, q],
             )
 
@@ -163,7 +166,7 @@ def tile_localconvolution_kernel(tc, x, weight, out):
         gather_windows(0)
         gather_windows(1)
 
-        done = GRP * EARLY_GROUPS
+        late = COLS * LATE_ROWS
         for t in range(NG + LEAD + 2):
             w = t - LEAD
             if t >= 2 and t % 2 == 0 and t // 2 - 1 < ROWS:
@@ -183,9 +186,9 @@ def tile_localconvolution_kernel(tc, x, weight, out):
                     flip_w(w, a)
                 if a == 1 and 0 <= w - 2 < NG:
                     multiply(w - 2)
-            if w - 2 == EARLY_GROUPS - 1:
-                nc.sync.dma_start(out=out_view[:, :, 0:done], in_=res[:, :, 0:done])
+            if w - 2 == NG - 2 * LATE_ROWS - 1:
+                nc.sync.dma_start(out=out_view[:, :, late:NPOS], in_=res[:, :, late:NPOS])
             if 0 <= w and w + WBUFS < NG:
                 load_w(w + WBUFS)
 
-        nc.sync.dma_start(out=out_view[:, :, done:NPOS], in_=res[:, :, done:NPOS])
+        nc.sync.dma_start(out=out_view[:, :, 0:late], in_=res[:, :, 0:late])

@@ -24,7 +24,10 @@ WBUFS = 5
 LEAD = 2
 HALF = P * SPAN
 XT_LEN = 2 * HALF + 64
-LATE_ROWS = 2
+SORTED = 2
+SORTED_GROUPS = 2
+ROW_ORDER = (4, 5, 6, 7, 2, 3, 0, 1)
+STORE_ROWS = {3: (4, 8), 5: (2, 4), 7: (0, 2)}
 FLOPS = 2 * NPOS * B * O * K
 
 
@@ -39,6 +42,7 @@ def tile_localconvolution_kernel(tc, x, weight, out):
         wraw_pool = ctx.enter_context(tc.tile_pool(name="wraw", bufs=WBUFS))
         gw_pool = ctx.enter_context(tc.tile_pool(name="gw", bufs=3))
         wq_pool = ctx.enter_context(tc.tile_pool(name="wq", bufs=8))
+        sorted_pool = ctx.enter_context(tc.tile_pool(name="sorted", bufs=2))
         pre_pool = ctx.enter_context(tc.tile_pool(name="pre", bufs=4))
         xt_pool = ctx.enter_context(tc.tile_pool(name="xt", bufs=3))
         sp_pool = ctx.enter_context(tc.tile_pool(name="sp", bufs=2))
@@ -60,15 +64,27 @@ def tile_localconvolution_kernel(tc, x, weight, out):
             in_=ident[:].rearrange("p (b g) -> p g b", g=2),
         )
 
-        wraw, gw, wc, ws, pre, xt, sp, pc, ps = {}, {}, {}, {}, {}, {}, {}, {}, {}
+        wraw, wsort, gw, wc, ws, pre, xt, sp, pc, ps = {}, {}, {}, {}, {}, {}, {}, {}, {}, {}
 
         def group(n):
-            return (n + 2 * LATE_ROWS) % NG
+            return 2 * ROW_ORDER[n // 2] + n % 2
+
+        def store(lo, hi):
+            nc.sync.dma_start(out=out_view[:, :, COLS * lo:COLS * hi], in_=res[:, :, COLS * lo:COLS * hi])
 
         def load_w(n):
             t = wraw_pool.tile([P, GRP, K], BF16, name="wraw")
             nc.sync.dma_start(out=t[:], in_=w_view[:, GRP * group(n):GRP * (group(n) + 1), :])
             wraw[n] = t
+
+        def sort_w(n):
+            t = sorted_pool.tile([P, SORTED, 4, P], F32, name="sorted")
+            wsort[n] = t
+            for a in range(SORTED):
+                nc.vector.tensor_copy(
+                    out=t[:, a].rearrange("p (g m) q -> p g m q", g=2),
+                    in_=wraw[n][:].bitcast(F32)[:, a].rearrange("p (g q m) -> p g m q", g=2, m=2),
+                )
 
         def flip_w(n, a):
             if a == 0:
@@ -78,8 +94,11 @@ def tile_localconvolution_kernel(tc, x, weight, out):
             bank = tp_pool.tile([P, 512], F32, name="tp")
             for s in range(4):
                 g, m = s // 2, s % 2
-                nc.tensor.transpose(bank[:, P * s:P * (s + 1)],
-                                    wf[:, a, 2 * P * g + m:2 * P * (g + 1):2], ident[:])
+                if n in wsort and a < SORTED:
+                    words = wsort[n][:, a, s]
+                else:
+                    words = wf[:, a, 2 * P * g + m:2 * P * (g + 1):2]
+                nc.tensor.transpose(bank[:, P * s:P * (s + 1)], words, ident[:])
             nc.scalar.copy(out=gf[:, a], in_=bank[:].rearrange("p (g m n) -> p g n m", g=2, m=2))
 
         def quantise_w(n, pair):
@@ -87,11 +106,15 @@ def tile_localconvolution_kernel(tc, x, weight, out):
             s_t = wq_pool.tile([P, 2 * 2 * O], U8, name="ws", align_bytes=64)
             wc[n, pair] = c_t
             ws[n, pair] = s_t
-            nc.vector.quantize_mx(
-                out=c_t[:].bitcast(FP8X4),
-                scales=s_t[:],
-                in_=gw[n][:, 2 * pair:2 * pair + 2].rearrange("p a g o t -> p (a g o t)"),
-            )
+            size = 1 if n == NG - 1 else 2
+            for k in range(0, 2, size):
+                cols = slice(2 * O * k, 2 * O * (k + size))
+                a = 2 * pair + k
+                nc.vector.quantize_mx(
+                    out=c_t[:, cols].bitcast(FP8X4),
+                    scales=s_t[:, cols],
+                    in_=gw[n][:, a:a + size].rearrange("p a g o t -> p (a g o t)"),
+                )
 
         def first_col(n):
             return (n % 2) * 3
@@ -166,7 +189,6 @@ def tile_localconvolution_kernel(tc, x, weight, out):
         gather_windows(0)
         gather_windows(1)
 
-        late = COLS * LATE_ROWS
         for t in range(NG + LEAD + 2):
             w = t - LEAD
             if t >= 2 and t % 2 == 0 and t // 2 - 1 < ROWS:
@@ -176,6 +198,8 @@ def tile_localconvolution_kernel(tc, x, weight, out):
                 quantise_p(t // 2 - 1, 1)
             if t + 2 < NG:
                 gather_windows(t + 2)
+            if NG - SORTED_GROUPS <= w + 1 < NG:
+                sort_w(w + 1)
             if t < NG:
                 flip_x(t)
             if 0 <= w - 1 < NG:
@@ -186,9 +210,7 @@ def tile_localconvolution_kernel(tc, x, weight, out):
                     flip_w(w, a)
                 if a == 1 and 0 <= w - 2 < NG:
                     multiply(w - 2)
-            if w - 2 == NG - 2 * LATE_ROWS - 1:
-                nc.sync.dma_start(out=out_view[:, :, late:NPOS], in_=res[:, :, late:NPOS])
             if 0 <= w and w + WBUFS < NG:
                 load_w(w + WBUFS)
-
-        nc.sync.dma_start(out=out_view[:, :, 0:late], in_=res[:, :, 0:late])
+            if w % 2 == 1 and w // 2 - 1 in STORE_ROWS:
+                store(*STORE_ROWS[w // 2 - 1])

from contextlib import ExitStack

import concourse.mybir as mybir
from concourse.masks import make_identity

F32 = mybir.dt.float32
BF16 = mybir.dt.bfloat16
I32 = mybir.dt.int32
U32 = mybir.dt.uint32
U8 = mybir.dt.uint8
FP8X4 = mybir.dt.float8_e4m3fn_x4

P = 128
B, C, O, ROWS, COLS, KH, KW = 64, 64, 128, 8, 8, 4, 4
H = 11
CH = C // 2
XLEN = CH * H * H
K = C * KH * KW
NPOS = ROWS * COLS
GRP = 4
NG = NPOS // GRP
SPAN = 8
WBUFS = 5
LEAD = 2
HALF = P * SPAN
XT_LEN = 2 * HALF + 64
SORTED = 2
SORTED_GROUPS = 2
ROW_ORDER = (4, 5, 6, 7, 2, 3, 0, 1)
STORE_ROWS = {3: (4, 8), 5: (2, 4), 7: (0, 2)}
FLOPS = 2 * NPOS * B * O * K


def tile_localconvolution_kernel(tc, x, weight, out):
    nc = tc.nc
    w_view = weight.rearrange("i j o c u v -> o (i j) (c u v)")
    x_view = x.rearrange("b (g c) h w -> (b g) (c h w)", g=2)
    out_view = out.rearrange("b o i j -> o b (i j)")

    with ExitStack() as ctx:
        keep = ctx.enter_context(tc.tile_pool(name="keep", bufs=1))
        wraw_pool = ctx.enter_context(tc.tile_pool(name="wraw", bufs=WBUFS))
        gw_pool = ctx.enter_context(tc.tile_pool(name="gw", bufs=3))
        wq_pool = ctx.enter_context(tc.tile_pool(name="wq", bufs=8))
        sorted_pool = ctx.enter_context(tc.tile_pool(name="sorted", bufs=2))
        pre_pool = ctx.enter_context(tc.tile_pool(name="pre", bufs=4))
        xt_pool = ctx.enter_context(tc.tile_pool(name="xt", bufs=3))
        sp_pool = ctx.enter_context(tc.tile_pool(name="sp", bufs=2))
        pq_pool = ctx.enter_context(tc.tile_pool(name="pq", bufs=3))
        tp_pool = ctx.enter_context(tc.psum_pool(name="tp", bufs=6))
        acc_pool = ctx.enter_context(tc.psum_pool(name="acc", bufs=2))
        ctx.enter_context(tc.manual_schedule())

        xs = keep.tile([P, XLEN], BF16, name="xs")
        nc.sync.dma_start(out=xs[:], in_=x_view)
        xs_img = xs[:].rearrange("p (c h w) -> p c h w", c=CH, h=H)

        ident = keep.tile([P, P], F32, name="ident")
        make_identity(nc, ident[:])
        perm = keep.tile([P, P], F32, name="perm")
        res = keep.tile([P, B, NPOS], F32, name="res")
        nc.vector.tensor_copy(
            out=perm[:].rearrange("p (g b) -> p g b", g=2),
            in_=ident[:].rearrange("p (b g) -> p g b", g=2),
        )

        wraw, wsort, gw, wc, ws, pre, xt, sp, pc, ps = {}, {}, {}, {}, {}, {}, {}, {}, {}, {}

        def group(n):
            return 2 * ROW_ORDER[n // 2] + n % 2

        def store(lo, hi):
            nc.sync.dma_start(out=out_view[:, :, COLS * lo:COLS * hi], in_=res[:, :, COLS * lo:COLS * hi])

        def load_w(n):
            t = wraw_pool.tile([P, GRP, K], BF16, name="wraw")
            nc.sync.dma_start(out=t[:], in_=w_view[:, GRP * group(n):GRP * (group(n) + 1), :])
            wraw[n] = t

        def sort_w(n):
            t = sorted_pool.tile([P, SORTED, 4, P], F32, name="sorted")
            wsort[n] = t
            for a in range(SORTED):
                nc.vector.tensor_copy(
                    out=t[:, a].rearrange("p (g m) q -> p g m q", g=2),
                    in_=wraw[n][:].bitcast(F32)[:, a].rearrange("p (g q m) -> p g m q", g=2, m=2),
                )

        def flip_w(n, a):
            if a == 0:
                gw[n] = gw_pool.tile([P, GRP, 2, O, 4], BF16, name="gw", align_bytes=64)
            wf = wraw[n][:].bitcast(F32)
            gf = gw[n][:].bitcast(F32)
            bank = tp_pool.tile([P, 512], F32, name="tp")
            for s in range(4):
                g, m = s // 2, s % 2
                if n in wsort and a < SORTED:
                    words = wsort[n][:, a, s]
                else:
                    words = wf[:, a, 2 * P * g + m:2 * P * (g + 1):2]
                nc.tensor.transpose(bank[:, P * s:P * (s + 1)], words, ident[:])
            nc.scalar.copy(out=gf[:, a], in_=bank[:].rearrange("p (g m n) -> p g n m", g=2, m=2))

        def quantise_w(n, pair):
            c_t = wq_pool.tile([P, 2 * 2 * O], U32, name="wc", align_bytes=64)
            s_t = wq_pool.tile([P, 2 * 2 * O], U8, name="ws", align_bytes=64)
            wc[n, pair] = c_t
            ws[n, pair] = s_t
            size = 1 if n == NG - 1 else 2
            for k in range(0, 2, size):
                cols = slice(2 * O * k, 2 * O * (k + size))
                a = 2 * pair + k
                nc.vector.quantize_mx(
                    out=c_t[:, cols].bitcast(FP8X4),
                    scales=s_t[:, cols],
                    in_=gw[n][:, a:a + size].rearrange("p a g o t -> p (a g o t)"),
                )

        def first_col(n):
            return (n % 2) * 3

        def gather_windows(n):
            i, w0 = group(n) // 2, first_col(n)
            t = pre_pool.tile([P, GRP, P, 2], BF16, name="pre")
            pre[n] = t
            nc.vector.tensor_copy(
                out=t[:].rearrange("p m (c u) e -> p c u m e", u=KH),
                in_=xs_img[:, :, i:i + KH, w0:w0 + SPAN].rearrange("p c u (m e) -> p c u m e", e=2),
            )

        def flip_x(n):
            i, h = n // 2, n % 2
            pf = pre[n][:].bitcast(F32).rearrange("p m q e -> p m (q e)")
            bank = tp_pool.tile([P, 512], F32, name="tp")
            for m in range(4):
                nc.tensor.transpose(bank[:, P * m:P * (m + 1)], pf[:, m], perm[:])
            if h == 0:
                xt[i] = xt_pool.tile([P, XT_LEN], BF16, name="xt", align_bytes=64)
            words = xt[i][:, HALF * h:HALF * (h + 1)].bitcast(F32).rearrange("p (n m) -> p n m", m=4)
            if h == 0:
                nc.scalar.copy(out=words, in_=bank[:].rearrange("p (m n) -> p n m", m=4))
            else:
                nc.vector.tensor_copy(out=words, in_=bank[:].rearrange("p (m n) -> p n m", m=4))

        def spread(i):
            t = sp_pool.tile([P, 2, P, 2, KW], BF16, name="sp", align_bytes=64)
            sp[i] = t
            for k in range(2):
                lo = k + 1
                nc.vector.tensor_copy(
                    out=t[:, k],
                    in_=xt[i][:, lo:lo + 2 * (HALF + 1)].rearrange("p (h x) -> p h x", h=2)[
                        :, :, 0:HALF].rearrange("p h (n e) -> p n h e", e=SPAN)[:, :, :, 0:KW],
                )

        def quantise_p(i, kind):
            if kind == 0:
                pc[i] = pq_pool.tile([P, 2, 4 * P], U32, name="pc", align_bytes=64)
                ps[i] = pq_pool.tile([P, 2, 4 * P], U8, name="ps", align_bytes=64)
                src = xt[i][:, 0:2 * HALF]
            else:
                src = sp[i][:].rearrange("p k n q v -> p (k n q v)")
            nc.vector.quantize_mx(out=pc[i][:, kind].bitcast(FP8X4), scales=ps[i][:, kind], in_=src)

        def multiply(n):
            i, q = n // 2, n % 2
            acc = acc_pool.tile([P, 512], F32, name="acc")
            for a in range(GRP):
                kind, k = ((0, 0), (1, 0), (1, 1), (0, 1))[a]
                for g in range(2):
                    lo = (2 * (a % 2) + g) * O
                    col = 2 * P * k + P * g
                    nc.tensor.matmul_mx(
                        out=acc[:, P * a:P * (a + 1)],
                        lhsT=wc[n, a // 2][:, lo:lo + O].bitcast(FP8X4),
                        lhsT_scale=ws[n, a // 2][:, lo:lo + O],
                        rhs=pc[i][:, kind, col:col + P].bitcast(FP8X4),
                        rhs_scale=ps[i][:, kind, col:col + P],
                        start=(g == 0),
                        stop=(g == 1),
                    )
            nc.scalar.copy(
                out=res[:, :, GRP * group(n):GRP * (group(n) + 1)],
                in_=acc[:].rearrange("p (a b q) -> p q b a", a=GRP, q=2)[:, q],
            )

        for n in range(WBUFS):
            load_w(n)
        gather_windows(0)
        gather_windows(1)

        for t in range(NG + LEAD + 2):
            w = t - LEAD
            if t >= 2 and t % 2 == 0 and t // 2 - 1 < ROWS:
                quantise_p(t // 2 - 1, 0)
                spread(t // 2 - 1)
            if t >= 3 and t % 2 == 1 and t // 2 - 1 < ROWS:
                quantise_p(t // 2 - 1, 1)
            if t + 2 < NG:
                gather_windows(t + 2)
            if NG - SORTED_GROUPS <= w + 1 < NG:
                sort_w(w + 1)
            if t < NG:
                flip_x(t)
            if 0 <= w - 1 < NG:
                quantise_w(w - 1, 0)
                quantise_w(w - 1, 1)
            for a in range(GRP):
                if 0 <= w < NG:
                    flip_w(w, a)
                if a == 1 and 0 <= w - 2 < NG:
                    multiply(w - 2)
            if 0 <= w and w + WBUFS < NG:
                load_w(w + WBUFS)
            if w % 2 == 1 and w // 2 - 1 in STORE_ROWS:
                store(*STORE_ROWS[w // 2 - 1])
